import numpy as np
import ml_dtypes


def mxq(x, axis, fmt="e4m3"):
    dtype, down = {"e4m3": (ml_dtypes.float8_e4m3fn, 7), "e5m2": (ml_dtypes.float8_e5m2, 14)}[fmt]
    v = np.moveaxis(np.asarray(x, np.float32).astype(ml_dtypes.bfloat16).astype(np.float64), axis, -1)
    blocks = v.reshape(v.shape[:-1] + (-1, 32))
    amax = np.abs(blocks).max(-1, keepdims=True)
    byte = np.maximum(np.where(amax > 0, np.frexp(amax)[1] - 1 + 127, 0) - down, 1)
    scale = np.exp2(byte - 127.0)
    codes = (blocks / scale).astype(np.float32).astype(dtype).astype(np.float64)
    return np.moveaxis((codes * scale).reshape(v.shape), -1, axis)


WIDE = False


def mx_kscale(k):
    if not WIDE:
        return np.ones(k)
    levels = np.array([10, -10, 5, -5, 0])
    a = np.random.permutation(np.resize(levels, k // 512 * 4)).reshape(k // 512, 4)
    idx = np.arange(k)
    return np.exp2(a[idx // 512, idx % 128 // 32])


BF16 = ml_dtypes.bfloat16


def bf(x):
    return np.asarray(x, np.float32).astype(BF16)


def f64(x):
    return np.asarray(x).astype(np.float64)


B, L, H, K = 4, 32, 1024, 128


def setup_inputs():
    u = np.exp2(np.round(np.log2(mx_kscale(H)) / 2))
    r = np.concatenate([u * u, u, u])
    return {"seq_out": bf(np.random.standard_normal((B, L, H)) * u),
            "W_proj": bf(np.random.standard_normal((3 * H, H)) * 0.5 / np.sqrt(H) / r[:, None]),
            "b_proj": bf(np.random.standard_normal(H) * 0.2),
            "W_out": bf(np.random.standard_normal((H, K)) * 1.5 / np.sqrt(H)),
            "b_out": bf(np.random.standard_normal(K) * 0.2)}


def reference(seq_out, W_proj, b_proj, W_out, b_out):
    x = f64(seq_out)
    W = f64(W_proj)
    W1, W2, W3 = W[:H], W[H:2 * H], W[2 * H:]
    p = x[:, :, None, :] * x[:, None, :, :]
    pw = mxq(p, 3, "e4m3") @ mxq(W1, 0, "e4m3")
    xq = mxq(x, 2, "e4m3")
    xi = (xq @ mxq(W2, 0, "e4m3"))[:, :, None, :]
    xj = (xq @ mxq(W3, 0, "e4m3"))[:, None, :, :]
    proj = np.tanh(pw + xi + xj + f64(b_proj))
    out = (mxq(proj, 3, "e4m3") @ mxq(f64(W_out), 0, "e4m3")) + f64(b_out)
    return out.transpose(0, 3, 1, 2)

@@ -1,0 +1,299 @@
+from contextlib import ExitStack
+
+import concourse.mybir as mybir
+from concourse.masks import make_identity
+
+FP8X4 = mybir.dt.float8_e4m3fn_x4
+BF16 = mybir.dt.bfloat16
+F32 = mybir.dt.float32
+U32 = mybir.dt.uint32
+U8 = mybir.dt.uint8
+I32 = mybir.dt.int32
+ACTF = mybir.ActivationFunctionType
+ALU = mybir.AluOpType
+
+P = 128
+B = 4
+L = 32
+H = 1024
+HALF = 16
+COLS = HALF * HALF
+
+FLOPS = 2 * B * L * L * H * H + 2 * 2 * B * L * H * H + 2 * B * L * L * H * P
+
+BLOCKS = ((0, 0, 0, False), (0, 1, 1, False), (0, 1, 1, True), (1, 1, 2, False))
+
+
+def tile_srlbertold_pa_kernel(tc, seq_out, W_proj, b_proj, W_out, b_out, out):
+    nc = tc.nc
+    with ExitStack() as ctx:
+        keep = ctx.enter_context(tc.tile_pool(name="keep", bufs=1))
+        wraw = ctx.enter_context(tc.tile_pool(name="wraw", bufs=6))
+        wgrp = ctx.enter_context(tc.tile_pool(name="wgrp", bufs=3))
+        prod = ctx.enter_context(tc.tile_pool(name="prod", bufs=3))
+        zpool = ctx.enter_context(tc.tile_pool(name="zpool", bufs=3))
+        jpool = ctx.enter_context(tc.tile_pool(name="jpool", bufs=3))
+        opool = ctx.enter_context(tc.tile_pool(name="opool", bufs=2))
+        psum = ctx.enter_context(tc.psum_pool(name="psum", bufs=6))
+        psum_o = ctx.enter_context(tc.psum_pool(name="psum_o", bufs=2))
+
+        ident = keep.tile([P, P], BF16)
+        x_sb = keep.tile([P, H], BF16)
+        bias_rows = keep.tile([P, P], BF16)
+        bias = keep.tile([P, 16], F32)
+        xg = keep.tile([P, 2, P, 4], BF16, align_bytes=64)
+        xc = keep.tile([P, 2, P], U32, align_bytes=64)
+        xs = keep.tile([P, 2, P], U8, align_bytes=64)
+        xec = keep.tile([P, 2, 8, HALF, HALF], U32, align_bytes=64)
+        xes = keep.tile([P, 2, 8, HALF, HALF], U8, align_bytes=64)
+        wc = [keep.tile([P, 2, H], U32, align_bytes=64, name="wc%d" % m) for m in range(3)]
+        ws = [keep.tile([P, 2, H], U8, align_bytes=64, name="ws%d" % m) for m in range(3)]
+        raw_o = keep.tile([P, 8, P], BF16)
+        grp_o = keep.tile([P, 2, P, 4], BF16, align_bytes=64)
+        oc = keep.tile([P, 2, P], U32, align_bytes=64)
+        os_ = keep.tile([P, 2, P], U8, align_bytes=64)
+        tab = [keep.tile([P, 8, P], F32, name="tab%d" % m) for m in range(2)]
+        pc = keep.tile([P, 12, 2, COLS], U32, align_bytes=64)
+        ps = keep.tile([P, 12, 2, COLS], U8, align_bytes=64)
+        jc = keep.tile([P, 16, 2, COLS], U32, align_bytes=64)
+        js = keep.tile([P, 16, 2, COLS], U8, align_bytes=64)
+
+        make_identity(nc, ident[:])
+        nc.sync.dma_start(out=x_sb[:], in_=seq_out.flatten_outer_dims())
+        nc.vector.memset(bias_rows[:], 0.0)
+        nc.vector.memset(xs[:].bitcast(I32), 0)
+        nc.scalar.dma_start(out=bias_rows[0:8, :], in_=b_proj.rearrange("(r c) -> r c", c=P))
+        nc.scalar.dma_start(out=bias_rows[8:9, :], in_=b_out.rearrange("(r c) -> r c", c=P))
+
+        def load_piece(m, c, g):
+            raw = wraw.tile([P, 4, 512], BF16, name="raw", tag="raw")
+            rows = W_proj[H * m + 512 * g : H * m + 512 * g + 512, 512 * c : 512 * c + 512]
+            nc.sync.dma_start(out=raw[:], in_=rows.rearrange("(t p) n -> p t n", p=P))
+            return raw
+
+        def pack_piece(raw, m, c, g, on_vector):
+            grp = wgrp.tile([P, 512, 4], BF16, align_bytes=64, name="grp", tag="grp")
+            dst = grp[:].rearrange("p (c i) t -> p c t i", i=4)
+            src = raw[:].rearrange("p t (c i) -> p c t i", i=4)
+            if on_vector:
+                nc.vector.tensor_copy(out=dst, in_=src)
+            else:
+                nc.scalar.copy(out=dst, in_=src)
+            nc.vector.quantize_mx(
+                out=wc[m][:, g, 512 * c : 512 * c + 512].bitcast(FP8X4),
+                scales=ws[m][:, g, 512 * c : 512 * c + 512],
+                in_=grp[:].rearrange("p n t -> p (n t)"),
+            )
+
+        first = [(0, 0, 0), (0, 0, 1), (2, 0, 0), (2, 0, 1), (1, 0, 0), (1, 0, 1)]
+        second = [(0, 1, 0), (0, 1, 1), (2, 1, 0), (2, 1, 1), (1, 1, 0), (1, 1, 1)]
+        raws = [load_piece(m, c, g) for (m, c, g) in first]
+
+        for g in range(2):
+            xt = psum.tile([P, 4, P], BF16, name="xt", tag="u")
+            for t in range(4):
+                k0 = 512 * g + P * t
+                nc.tensor.transpose(xt[:, t, :], x_sb[:, k0 : k0 + P], ident[:])
+            nc.scalar.copy(out=xg[:, g], in_=xt[:].rearrange("p t r -> p r t"))
+        bt = psum.tile([P, P], BF16, name="bt", tag="u")
+        nc.tensor.transpose(bt[:], bias_rows[:], ident[:])
+        nc.vector.tensor_copy(out=bias[:], in_=bt[:, 0:16])
+        nc.vector.quantize_mx(
+            out=xc[:].rearrange("p g r -> p (g r)").bitcast(FP8X4),
+            scales=xs[:].rearrange("p g r -> p (g r)"),
+            in_=xg[:].rearrange("p g r t -> p (g r t)"),
+        )
+
+        def expand_x(b):
+            for g in range(2):
+                nc.vector.tensor_copy(
+                    out=xec[:, g, 2 * b : 2 * b + 2].bitcast(I32),
+                    in_=xc[:, g, L * b : L * b + L]
+                    .bitcast(I32)
+                    .rearrange("p (s m) -> p s m", m=HALF)
+                    .unsqueeze(2)
+                    .to_broadcast([P, 2, HALF, HALF]),
+                )
+                nc.vector.tensor_copy(
+                    out=xes[:, g, 2 * b : 2 * b + 2].bitcast(I32),
+                    in_=xs[:, g, L * b : L * b + L]
+                    .bitcast(I32)
+                    .rearrange("p (s m) -> p s m", m=HALF // 4)
+                    .unsqueeze(2)
+                    .to_broadcast([P, 2, HALF, HALF // 4]),
+                )
+
+        def product(b, pidx):
+            i_half, j_half = ((0, 0), (0, 1), (1, 1))[pidx]
+            pr = prod.tile([P, 2, HALF, HALF, 4], BF16, align_bytes=64, name="pr", tag="pr")
+            t_major = L * b + HALF * i_half
+            t_minor = L * b + HALF * j_half
+            for g in range(2):
+                nc.vector.tensor_tensor(
+                    out=pr[:, g],
+                    in0=xg[:, g, t_major : t_major + HALF, :]
+                    .unsqueeze(2)
+                    .to_broadcast([P, HALF, HALF, 4]),
+                    in1=xg[:, g, t_minor : t_minor + HALF, :]
+                    .unsqueeze(1)
+                    .to_broadcast([P, HALF, HALF, 4]),
+                    op=ALU.mult,
+                )
+            nc.vector.quantize_mx(
+                out=pc[:, 3 * b + pidx].rearrange("p g c -> p (g c)").bitcast(FP8X4),
+                scales=ps[:, 3 * b + pidx].rearrange("p g c -> p (g c)"),
+                in_=pr[:].rearrange("p g a m t -> p (g a m t)"),
+            )
+
+        def tables(gh):
+            for ti, m in ((0, 1), (1, 2)):
+                tp = psum.tile([P, 4, P], F32, name="tp", tag="u")
+                for t in range(4):
+                    h0 = 512 * gh + P * t
+                    for g in range(2):
+                        nc.tensor.matmul_mx(
+                            out=tp[:, t, :],
+                            lhsT=wc[m][:, g, h0 : h0 + P].bitcast(FP8X4),
+                            lhsT_scale=ws[m][:, g, h0 : h0 + P],
+                            rhs=xc[:, g, :].bitcast(FP8X4),
+                            rhs_scale=xs[:, g, :],
+                            start=(g == 0),
+                            stop=(g == 1),
+                        )
+                nc.vector.tensor_tensor(
+                    out=tab[ti][:, 4 * gh : 4 * gh + 4, :],
+                    in0=tp[:],
+                    in1=bias[:, 4 * gh : 4 * gh + 4].unsqueeze(2).to_broadcast([P, 4, P]),
+                    op=ALU.add,
+                )
+
+        def pack_w_out():
+            nc.scalar.copy(out=grp_o[:], in_=raw_o[:].rearrange("p (g t) n -> p g n t", t=4))
+            nc.vector.quantize_mx(
+                out=oc[:].rearrange("p g n -> p (g n)").bitcast(FP8X4),
+                scales=os_[:].rearrange("p g n -> p (g n)"),
+                in_=grp_o[:].rearrange("p g n t -> p (g n t)"),
+            )
+
+        def unit(tau, gh):
+            b = tau // 4
+            i_half, j_half, pidx, mirrored = BLOCKS[tau % 4]
+            m_in = 1 if mirrored else 2
+            table = tab[1] if mirrored else tab[0]
+            t_major = L * b + HALF * i_half
+            slot = 2 * b + j_half
+            z = zpool.tile([P, 2, COLS, 2], F32, name="z", tag="z")
+            for q in range(2):
+                bank = psum.tile([P, 2, COLS], F32, name="bank", tag="u")
+                for u in range(2):
+                    h0 = 512 * gh + P * (2 * q + u)
+                    for g in range(2):
+                        nc.tensor.matmul_mx(
+                            out=bank[:, u, :],
+                            lhsT=wc[0][:, g, h0 : h0 + P].bitcast(FP8X4),
+                            lhsT_scale=ws[0][:, g, h0 : h0 + P],
+                            rhs=pc[:, 3 * b + pidx, g, :].bitcast(FP8X4),
+                            rhs_scale=ps[:, 3 * b + pidx, g, :],
+                            start=(g == 0),
+                            stop=False,
+                        )
+                    for g in range(2):
+                        nc.tensor.matmul_mx(
+                            out=bank[:, u, :],
+                            lhsT=wc[m_in][:, g, h0 : h0 + P].bitcast(FP8X4),
+                            lhsT_scale=ws[m_in][:, g, h0 : h0 + P],
+                            rhs=xec[:, g, slot].rearrange("p a m -> p (a m)").bitcast(FP8X4),
+                            rhs_scale=xes[:, g, slot].rearrange("p a m -> p (a m)"),
+                            start=False,
+                            stop=(g == 1),
+                        )
+                plane = 4 * gh + 2 * q
+                nc.vector.tensor_tensor(
+                    out=z[:, q].rearrange("p (a m) u -> p a m u", m=HALF),
+                    in0=bank[:].rearrange("p u (a m) -> p a m u", m=HALF),
+                    in1=table[:, plane : plane + 2, t_major : t_major + HALF]
+                    .rearrange("p u a -> p a u")
+                    .unsqueeze(2)
+                    .to_broadcast([P, HALF, HALF, 2]),
+                    op=ALU.add,
+                )
+            pj = jpool.tile([P, COLS, 4], BF16, align_bytes=64, name="pj", tag="pj")
+            nc.scalar.activation(
+                out=pj[:].rearrange("p c (q u) -> p c q u", u=2),
+                in_=z[:].rearrange("p q c u -> p c q u"),
+                func=ACTF.Tanh,
+            )
+            nc.vector.quantize_mx(
+                out=jc[:, tau, gh, :].bitcast(FP8X4),
+                scales=js[:, tau, gh, :],
+                in_=pj[:].rearrange("p c t -> p (c t)"),
+            )
+
+        def labels(tau, o_sb):
+            i_half, j_half, pidx, mirrored = BLOCKS[tau % 4]
+            ob = psum_o.tile([P, COLS], F32, name="ob", tag="o")
+            for gh in range(2):
+                nc.tensor.matmul_mx(
+                    out=ob[:],
+                    lhsT=oc[:, gh, :].bitcast(FP8X4),
+                    lhsT_scale=os_[:, gh, :],
+                    rhs=jc[:, tau, gh, :].bitcast(FP8X4),
+                    rhs_scale=js[:, tau, gh, :],
+                    start=(gh == 0),
+                    stop=(gh == 1),
+                )
+            if mirrored:
+                dst = o_sb[:, HALF * j_half : HALF * j_half + HALF, HALF * i_half : HALF * i_half + HALF]
+                src = ob[:].rearrange("p (a m) -> p m a", m=HALF)
+            else:
+                dst = o_sb[:, HALF * i_half : HALF * i_half + HALF, HALF * j_half : HALF * j_half + HALF]
+                src = ob[:].rearrange("p (a m) -> p a m", m=HALF)
+            nc.scalar.activation(out=dst, in_=src, func=ACTF.Identity, bias=bias[:, 8:9], scale=1.0)
+
+        expand_x(0)
+        product(0, 0)
+        product(0, 1)
+        raws2 = []
+        for n, (m, c, g) in enumerate(first):
+            pack_piece(raws[n], m, c, g, on_vector=(g == 0))
+            raws2.append(load_piece(*second[n]))
+        nc.sync.dma_start(out=raw_o[:], in_=W_out.rearrange("(a p) n -> p a n", p=P))
+        tables(0)
+
+        order = [(t, 0) for t in range(8)]
+        for t in range(8):
+            order.append((t, 1))
+            order.append((t + 8, 0))
+        for t in range(8, 16):
+            order.append((t, 1))
+
+        made = set([(0, 0), (0, 1)])
+        expanded = set([0])
+        o_tiles = {}
+        for n, (tau, gh) in enumerate(order):
+            for tau2, gh2 in order[n : n + 3]:
+                b2 = tau2 // 4
+                key = (b2, BLOCKS[tau2 % 4][2])
+                if b2 not in expanded:
+                    expand_x(b2)
+                    expanded.add(b2)
+                if key not in made:
+                    product(b2, key[1])
+                    made.add(key)
+            unit(tau, gh)
+            if n < 6:
+                m, c, g = second[n]
+                pack_piece(raws2[n], m, c, g, on_vector=False)
+            if n == 6:
+                tables(1)
+                pack_w_out()
+            if gh == 1:
+                b = tau // 4
+                if b not in o_tiles:
+                    o_tiles[b] = opool.tile([P, L, L], F32, name="o_sb", tag="o_sb")
+                labels(tau, o_tiles[b])
+                if tau % 4 == 3:
+                    nc.sync.dma_start(
+                        out=out[b].rearrange("k i j -> k (i j)"),
+                        in_=o_tiles[b][:].rearrange("p i j -> p (i j)"),
+                    )

@@ -21,7 +21,8 @@ COLS = HALF * HALF
 
 FLOPS = 2 * B * L * L * H * H + 2 * 2 * B * L * H * H + 2 * B * L * L * H * P
 
-BLOCKS = ((0, 0, 0, False), (0, 1, 1, False), (0, 1, 1, True), (1, 1, 2, False))
+BLOCKS = ((0, 0), (0, 1), (1, 1))
+OWN_GROUP = (0,)
 
 
 def tile_srlbertold_pa_kernel(tc, seq_out, W_proj, b_proj, W_out, b_out, out):
@@ -32,6 +33,7 @@ def tile_srlbertold_pa_kernel(tc, seq_out, W_proj, b_proj, W_out, b_out, out):
         wgrp = ctx.enter_context(tc.tile_pool(name="wgrp", bufs=3))
         prod = ctx.enter_context(tc.tile_pool(name="prod", bufs=3))
         zpool = ctx.enter_context(tc.tile_pool(name="zpool", bufs=3))
+        spool = ctx.enter_context(tc.tile_pool(name="spool", bufs=2))
         jpool = ctx.enter_context(tc.tile_pool(name="jpool", bufs=3))
         opool = ctx.enter_context(tc.tile_pool(name="opool", bufs=2))
         psum = ctx.enter_context(tc.psum_pool(name="psum", bufs=6))
@@ -52,7 +54,9 @@ def tile_srlbertold_pa_kernel(tc, seq_out, W_proj, b_proj, W_out, b_out, out):
         grp_o = keep.tile([P, 2, P, 4], BF16, align_bytes=64)
         oc = keep.tile([P, 2, P], U32, align_bytes=64)
         os_ = keep.tile([P, 2, P], U8, align_bytes=64)
-        tab = [keep.tile([P, 8, P], F32, name="tab%d" % m) for m in range(2)]
+        tab_a = keep.tile([P, 8, P], F32)
+        tab_c = keep.tile([P, 8, P], F32)
+        tab_d = keep.tile([P, 8, P], F32)
         pc = keep.tile([P, 12, 2, COLS], U32, align_bytes=64)
         ps = keep.tile([P, 12, 2, COLS], U8, align_bytes=64)
         jc = keep.tile([P, 16, 2, COLS], U32, align_bytes=64)
@@ -98,33 +102,34 @@ def tile_srlbertold_pa_kernel(tc, seq_out, W_proj, b_proj, W_out, b_out, out):
         bt = psum.tile([P, P], BF16, name="bt", tag="u")
         nc.tensor.transpose(bt[:], bias_rows[:], ident[:])
         nc.vector.tensor_copy(out=bias[:], in_=bt[:, 0:16])
-        nc.vector.quantize_mx(
-            out=xc[:].rearrange("p g r -> p (g r)").bitcast(FP8X4),
-            scales=xs[:].rearrange("p g r -> p (g r)"),
-            in_=xg[:].rearrange("p g r t -> p (g r t)"),
-        )
+
+        def quantise_x():
+            nc.vector.quantize_mx(
+                out=xc[:].rearrange("p g r -> p (g r)").bitcast(FP8X4),
+                scales=xs[:].rearrange("p g r -> p (g r)"),
+                in_=xg[:].rearrange("p g r t -> p (g r t)"),
+            )
 
         def expand_x(b):
-            for g in range(2):
-                nc.vector.tensor_copy(
-                    out=xec[:, g, 2 * b : 2 * b + 2].bitcast(I32),
-                    in_=xc[:, g, L * b : L * b + L]
-                    .bitcast(I32)
-                    .rearrange("p (s m) -> p s m", m=HALF)
-                    .unsqueeze(2)
-                    .to_broadcast([P, 2, HALF, HALF]),
-                )
-                nc.vector.tensor_copy(
-                    out=xes[:, g, 2 * b : 2 * b + 2].bitcast(I32),
-                    in_=xs[:, g, L * b : L * b + L]
-                    .bitcast(I32)
-                    .rearrange("p (s m) -> p s m", m=HALF // 4)
-                    .unsqueeze(2)
-                    .to_broadcast([P, 2, HALF, HALF // 4]),
-                )
+            nc.vector.tensor_copy(
+                out=xec[:, :, 2 * b : 2 * b + 2].bitcast(I32),
+                in_=xc[:, :, L * b : L * b + L]
+                .bitcast(I32)
+                .rearrange("p g (s m) -> p g s m", m=HALF)
+                .unsqueeze(3)
+                .to_broadcast([P, 2, 2, HALF, HALF]),
+            )
+            nc.vector.tensor_copy(
+                out=xes[:, :, 2 * b : 2 * b + 2].bitcast(I32),
+                in_=xs[:, :, L * b : L * b + L]
+                .bitcast(I32)
+                .rearrange("p g (s m) -> p g s m", m=HALF // 4)
+                .unsqueeze(3)
+                .to_broadcast([P, 2, 2, HALF, HALF // 4]),
+            )
 
-        def product(b, pidx):
-            i_half, j_half = ((0, 0), (0, 1), (1, 1))[pidx]
+        def product(b, blk):
+            i_half, j_half = BLOCKS[blk]
             pr = prod.tile([P, 2, HALF, HALF, 4], BF16, align_bytes=64, name="pr", tag="pr")
             t_major = L * b + HALF * i_half
             t_minor = L * b + HALF * j_half
@@ -140,13 +145,13 @@ def tile_srlbertold_pa_kernel(tc, seq_out, W_proj, b_proj, W_out, b_out, out):
                     op=ALU.mult,
                 )
             nc.vector.quantize_mx(
-                out=pc[:, 3 * b + pidx].rearrange("p g c -> p (g c)").bitcast(FP8X4),
-                scales=ps[:, 3 * b + pidx].rearrange("p g c -> p (g c)"),
+                out=pc[:, 3 * b + blk].rearrange("p g c -> p (g c)").bitcast(FP8X4),
+                scales=ps[:, 3 * b + blk].rearrange("p g c -> p (g c)"),
                 in_=pr[:].rearrange("p g a m t -> p (g a m t)"),
             )
 
         def tables(gh):
-            for ti, m in ((0, 1), (1, 2)):
+            for table, m in ((tab_a, 1), (tab_c, 2)):
                 tp = psum.tile([P, 4, P], F32, name="tp", tag="u")
                 for t in range(4):
                     h0 = 512 * gh + P * t
@@ -160,11 +165,21 @@ def tile_srlbertold_pa_kernel(tc, seq_out, W_proj, b_proj, W_out, b_out, out):
                             start=(g == 0),
                             stop=(g == 1),
                         )
+                for t in range(4):
+                    plane = 4 * gh + t
+                    nc.scalar.activation(
+                        out=table[:, plane, :],
+                        in_=tp[:, t, :],
+                        func=ACTF.Identity,
+                        bias=bias[:, plane : plane + 1],
+                        scale=1.0,
+                    )
+            if gh not in OWN_GROUP:
                 nc.vector.tensor_tensor(
-                    out=tab[ti][:, 4 * gh : 4 * gh + 4, :],
-                    in0=tp[:],
-                    in1=bias[:, 4 * gh : 4 * gh + 4].unsqueeze(2).to_broadcast([P, 4, P]),
-                    op=ALU.add,
+                    out=tab_d[:, 4 * gh : 4 * gh + 4, :],
+                    in0=tab_a[:, 4 * gh : 4 * gh + 4, :],
+                    in1=tab_c[:, 4 * gh : 4 * gh + 4, :],
+                    op=ALU.subtract,
                 )
 
         def pack_w_out():
@@ -175,14 +190,17 @@ def tile_srlbertold_pa_kernel(tc, seq_out, W_proj, b_proj, W_out, b_out, out):
                 in_=grp_o[:].rearrange("p g n t -> p (g n t)"),
             )
 
-        def unit(tau, gh):
-            b = tau // 4
-            i_half, j_half, pidx, mirrored = BLOCKS[tau % 4]
-            m_in = 1 if mirrored else 2
-            table = tab[1] if mirrored else tab[0]
-            t_major = L * b + HALF * i_half
-            slot = 2 * b + j_half
-            z = zpool.tile([P, 2, COLS, 2], F32, name="z", tag="z")
+        def of_major(table, plane, token):
+            view = table[:, plane : plane + 2, token : token + HALF].rearrange("p u a -> p a u")
+            return view.unsqueeze(2).to_broadcast([P, HALF, HALF, 2])
+
+        def of_minor(table, plane, token):
+            view = table[:, plane : plane + 2, token : token + HALF].rearrange("p u m -> p m u")
+            return view.unsqueeze(1).to_broadcast([P, HALF, HALF, 2])
+
+        def pair_sums(b, blk, gh, m_in):
+            slot = 2 * b + BLOCKS[blk][1]
+            banks = []
             for q in range(2):
                 bank = psum.tile([P, 2, COLS], F32, name="bank", tag="u")
                 for u in range(2):
@@ -192,8 +210,8 @@ def tile_srlbertold_pa_kernel(tc, seq_out, W_proj, b_proj, W_out, b_out, out):
                             out=bank[:, u, :],
                             lhsT=wc[0][:, g, h0 : h0 + P].bitcast(FP8X4),
                             lhsT_scale=ws[0][:, g, h0 : h0 + P],
-                            rhs=pc[:, 3 * b + pidx, g, :].bitcast(FP8X4),
-                            rhs_scale=ps[:, 3 * b + pidx, g, :],
+                            rhs=pc[:, 3 * b + blk, g, :].bitcast(FP8X4),
+                            rhs_scale=ps[:, 3 * b + blk, g, :],
                             start=(g == 0),
                             stop=False,
                         )
@@ -207,14 +225,16 @@ def tile_srlbertold_pa_kernel(tc, seq_out, W_proj, b_proj, W_out, b_out, out):
                             start=False,
                             stop=(g == 1),
                         )
-                plane = 4 * gh + 2 * q
+                banks.append(bank)
+            return banks
+
+        def squash(banks, addends, tau, gh):
+            z = zpool.tile([P, 2, COLS, 2], F32, name="z", tag="z")
+            for q in range(2):
                 nc.vector.tensor_tensor(
                     out=z[:, q].rearrange("p (a m) u -> p a m u", m=HALF),
-                    in0=bank[:].rearrange("p u (a m) -> p a m u", m=HALF),
-                    in1=table[:, plane : plane + 2, t_major : t_major + HALF]
-                    .rearrange("p u a -> p a u")
-                    .unsqueeze(2)
-                    .to_broadcast([P, HALF, HALF, 2]),
+                    in0=banks[q][:].rearrange("p u (a m) -> p a m u", m=HALF),
+                    in1=addends[q],
                     op=ALU.add,
                 )
             pj = jpool.tile([P, COLS, 4], BF16, align_bytes=64, name="pj", tag="pj")
@@ -229,8 +249,31 @@ def tile_srlbertold_pa_kernel(tc, seq_out, W_proj, b_proj, W_out, b_out, out):
                 in_=pj[:].rearrange("p c t -> p (c t)"),
             )
 
+        def unit(b, blk, gh):
+            i_half, j_half = BLOCKS[blk]
+            t_major = L * b + HALF * i_half
+            t_minor = L * b + HALF * j_half
+            planes = (4 * gh, 4 * gh + 2)
+            banks = pair_sums(b, blk, gh, 2)
+            squash(banks, [of_major(tab_a, pl, t_major) for pl in planes], 4 * b + (0, 1, 3)[blk], gh)
+            if blk != 1:
+                return
+            if gh in OWN_GROUP:
+                banks = pair_sums(b, blk, gh, 1)
+                squash(banks, [of_major(tab_c, pl, t_major) for pl in planes], 4 * b + 2, gh)
+            else:
+                s2 = spool.tile([P, 2, COLS, 2], F32, name="s2", tag="s2")
+                views = [s2[:, q].rearrange("p (a m) u -> p a m u", m=HALF) for q in range(2)]
+                for q in range(2):
+                    nc.vector.tensor_tensor(
+                        out=views[q],
+                        in0=of_major(tab_c, planes[q], t_major),
+                        in1=of_minor(tab_d, planes[q], t_minor),
+                        op=ALU.add,
+                    )
+                squash(banks, views, 4 * b + 2, gh)
+
         def labels(tau, o_sb):
-            i_half, j_half, pidx, mirrored = BLOCKS[tau % 4]
             ob = psum_o.tile([P, COLS], F32, name="ob", tag="o")
             for gh in range(2):
                 nc.tensor.matmul_mx(
@@ -242,58 +285,64 @@ def tile_srlbertold_pa_kernel(tc, seq_out, W_proj, b_proj, W_out, b_out, out):
                     start=(gh == 0),
                     stop=(gh == 1),
                 )
-            if mirrored:
-                dst = o_sb[:, HALF * j_half : HALF * j_half + HALF, HALF * i_half : HALF * i_half + HALF]
+            kind = tau % 4
+            row0 = HALF * (kind // 2)
+            col0 = HALF * (kind % 2)
+            if kind == 2:
                 src = ob[:].rearrange("p (a m) -> p m a", m=HALF)
             else:
-                dst = o_sb[:, HALF * i_half : HALF * i_half + HALF, HALF * j_half : HALF * j_half + HALF]
                 src = ob[:].rearrange("p (a m) -> p a m", m=HALF)
-            nc.scalar.activation(out=dst, in_=src, func=ACTF.Identity, bias=bias[:, 8:9], scale=1.0)
+            nc.scalar.activation(
+                out=o_sb[:, row0 : row0 + HALF, col0 : col0 + HALF],
+                in_=src,
+                func=ACTF.Identity,
+                bias=bias[:, 8:9],
+                scale=1.0,
+            )
 
-        expand_x(0)
+        pack_piece(raws[0], *first[0], on_vector=True)
+        quantise_x()
+        pack_piece(raws[1], *first[1], on_vector=False)
         product(0, 0)
-        product(0, 1)
-        raws2 = []
-        for n, (m, c, g) in enumerate(first):
-            pack_piece(raws[n], m, c, g, on_vector=(g == 0))
-            raws2.append(load_piece(*second[n]))
+        pack_piece(raws[2], *first[2], on_vector=True)
+        pack_piece(raws[3], *first[3], on_vector=False)
+        expand_x(0)
+        pack_piece(raws[4], *first[4], on_vector=False)
+        pack_piece(raws[5], *first[5], on_vector=False)
+        raws2 = [load_piece(m, c, g) for (m, c, g) in second]
         nc.sync.dma_start(out=raw_o[:], in_=W_out.rearrange("(a p) n -> p a n", p=P))
         tables(0)
 
-        order = [(t, 0) for t in range(8)]
-        for t in range(8):
-            order.append((t, 1))
-            order.append((t + 8, 0))
-        for t in range(8, 16):
-            order.append((t, 1))
+        order = [(b, blk, 0) for b in range(2) for blk in range(3)]
+        order += [(b, blk, 1) for b in range(2) for blk in range(3)]
+        order += [(b, blk, gh) for b in range(2, 4) for blk in range(3) for gh in range(2)]
 
-        made = set([(0, 0), (0, 1)])
+        made = set([(0, 0)])
         expanded = set([0])
         o_tiles = {}
-        for n, (tau, gh) in enumerate(order):
-            for tau2, gh2 in order[n : n + 3]:
-                b2 = tau2 // 4
-                key = (b2, BLOCKS[tau2 % 4][2])
+        for n, (b, blk, gh) in enumerate(order):
+            for b2, blk2, gh2 in order[n : n + 3]:
+                if (b2, blk2) not in made:
+                    product(b2, blk2)
+                    made.add((b2, blk2))
                 if b2 not in expanded:
                     expand_x(b2)
                     expanded.add(b2)
-                if key not in made:
-                    product(b2, key[1])
-                    made.add(key)
-            unit(tau, gh)
-            if n < 6:
-                m, c, g = second[n]
-                pack_piece(raws2[n], m, c, g, on_vector=False)
-            if n == 6:
-                tables(1)
+            unit(b, blk, gh)
+            if n == 0:
+                for k, (m, c, g) in enumerate(second):
+                    pack_piece(raws2[k], m, c, g, on_vector=False)
                 pack_w_out()
+            if n == 4:
+                tables(1)
             if gh == 1:
-                b = tau // 4
                 if b not in o_tiles:
                     o_tiles[b] = opool.tile([P, L, L], F32, name="o_sb", tag="o_sb")
-                labels(tau, o_tiles[b])
-                if tau % 4 == 3:
+                for tau in ((0,), (1, 2), (3,))[blk]:
+                    labels(4 * b + tau, o_tiles[b])
+                if blk >= 1:
+                    r0 = HALF * (blk // 2)
                     nc.sync.dma_start(
-                        out=out[b].rearrange("k i j -> k (i j)"),
-                        in_=o_tiles[b][:].rearrange("p i j -> p (i j)"),
+                        out=out[b, :, r0 : r0 + HALF, :].rearrange("k i j -> k (i j)"),
+                        in_=o_tiles[b][:, r0 : r0 + HALF, :].rearrange("p i j -> p (i j)"),
                     )

@@ -16,12 +16,12 @@ P = 128
 B = 4
 L = 32
 H = 1024
-HALF = 16
-COLS = HALF * HALF
+Q = 8
+COLS = Q * Q * B
 
 FLOPS = 2 * B * L * L * H * H + 2 * 2 * B * L * H * H + 2 * B * L * L * H * P
 
-BLOCKS = ((0, 0), (0, 1), (1, 1))
+BLOCKS = [(i, j) for i in range(4) for j in range(i, 4)]
 OWN_GROUP = (0,)
 
 
@@ -35,7 +35,6 @@ def tile_srlbertold_pa_kernel(tc, seq_out, W_proj, b_proj, W_out, b_out, out):
         zpool = ctx.enter_context(tc.tile_pool(name="zpool", bufs=3))
         spool = ctx.enter_context(tc.tile_pool(name="spool", bufs=2))
         jpool = ctx.enter_context(tc.tile_pool(name="jpool", bufs=3))
-        opool = ctx.enter_context(tc.tile_pool(name="opool", bufs=2))
         psum = ctx.enter_context(tc.psum_pool(name="psum", bufs=6))
         psum_o = ctx.enter_context(tc.psum_pool(name="psum_o", bufs=2))
 
@@ -43,11 +42,11 @@ def tile_srlbertold_pa_kernel(tc, seq_out, W_proj, b_proj, W_out, b_out, out):
         x_sb = keep.tile([P, H], BF16)
         bias_rows = keep.tile([P, P], BF16)
         bias = keep.tile([P, 16], F32)
-        xg = keep.tile([P, 2, P, 4], BF16, align_bytes=64)
+        xg = keep.tile([P, 2, L, B * 4], BF16, align_bytes=64)
         xc = keep.tile([P, 2, P], U32, align_bytes=64)
         xs = keep.tile([P, 2, P], U8, align_bytes=64)
-        xec = keep.tile([P, 2, 8, HALF, HALF], U32, align_bytes=64)
-        xes = keep.tile([P, 2, 8, HALF, HALF], U8, align_bytes=64)
+        xec = keep.tile([P, 2, L, Q, B], U32, align_bytes=64)
+        xes = keep.tile([P, 2, L, Q, B], U8, align_bytes=64)
         wc = [keep.tile([P, 2, H], U32, align_bytes=64, name="wc%d" % m) for m in range(3)]
         ws = [keep.tile([P, 2, H], U8, align_bytes=64, name="ws%d" % m) for m in range(3)]
         raw_o = keep.tile([P, 8, P], BF16)
@@ -56,11 +55,12 @@ def tile_srlbertold_pa_kernel(tc, seq_out, W_proj, b_proj, W_out, b_out, out):
         os_ = keep.tile([P, 2, P], U8, align_bytes=64)
         tab_a = keep.tile([P, 8, P], F32)
         tab_c = keep.tile([P, 8, P], F32)
-        tab_d = keep.tile([P, 8, P], F32)
-        pc = keep.tile([P, 12, 2, COLS], U32, align_bytes=64)
-        ps = keep.tile([P, 12, 2, COLS], U8, align_bytes=64)
+        tab_e = keep.tile([P, 2, 2, P, 2], F32)
+        pc = keep.tile([P, 10, 2, COLS], U32, align_bytes=64)
+        ps = keep.tile([P, 10, 2, COLS], U8, align_bytes=64)
         jc = keep.tile([P, 16, 2, COLS], U32, align_bytes=64)
         js = keep.tile([P, 16, 2, COLS], U8, align_bytes=64)
+        o_sb = keep.tile([P, B, L, L], F32)
 
         make_identity(nc, ident[:])
         nc.sync.dma_start(out=x_sb[:], in_=seq_out.flatten_outer_dims())
@@ -89,8 +89,8 @@ def tile_srlbertold_pa_kernel(tc, seq_out, W_proj, b_proj, W_out, b_out, out):
                 in_=grp[:].rearrange("p n t -> p (n t)"),
             )
 
-        first = [(0, 0, 0), (0, 0, 1), (2, 0, 0), (2, 0, 1), (1, 0, 0), (1, 0, 1)]
-        second = [(0, 1, 0), (0, 1, 1), (2, 1, 0), (2, 1, 1), (1, 1, 0), (1, 1, 1)]
+        first = [(0, 0, 0), (0, 0, 1), (1, 0, 0), (1, 0, 1), (2, 0, 0), (2, 0, 1)]
+        second = [(0, 1, 0), (0, 1, 1), (1, 1, 0), (1, 1, 1), (2, 1, 0), (2, 1, 1)]
         raws = [load_piece(m, c, g) for (m, c, g) in first]
 
         for g in range(2):
@@ -98,7 +98,10 @@ def tile_srlbertold_pa_kernel(tc, seq_out, W_proj, b_proj, W_out, b_out, out):
             for t in range(4):
                 k0 = 512 * g + P * t
                 nc.tensor.transpose(xt[:, t, :], x_sb[:, k0 : k0 + P], ident[:])
-            nc.scalar.copy(out=xg[:, g], in_=xt[:].rearrange("p t r -> p r t"))
+            nc.scalar.copy(
+                out=xg[:, g].rearrange("p l (b t) -> p l b t", b=B),
+                in_=xt[:].rearrange("p t (b l) -> p l b t", b=B),
+            )
         bt = psum.tile([P, P], BF16, name="bt", tag="u")
         nc.tensor.transpose(bt[:], bias_rows[:], ident[:])
         nc.vector.tensor_copy(out=bias[:], in_=bt[:, 0:16])
@@ -107,51 +110,45 @@ def tile_srlbertold_pa_kernel(tc, seq_out, W_proj, b_proj, W_out, b_out, out):
             nc.vector.quantize_mx(
                 out=xc[:].rearrange("p g r -> p (g r)").bitcast(FP8X4),
                 scales=xs[:].rearrange("p g r -> p (g r)"),
-                in_=xg[:].rearrange("p g r t -> p (g r t)"),
+                in_=xg[:].rearrange("p g l k -> p (g l k)"),
             )
 
-        def expand_x(b):
+        def expand_x():
             nc.vector.tensor_copy(
-                out=xec[:, :, 2 * b : 2 * b + 2].bitcast(I32),
-                in_=xc[:, :, L * b : L * b + L]
+                out=xec[:].bitcast(I32).rearrange("p g l m b -> p (g l) m b"),
+                in_=xc[:]
                 .bitcast(I32)
-                .rearrange("p g (s m) -> p g s m", m=HALF)
-                .unsqueeze(3)
-                .to_broadcast([P, 2, 2, HALF, HALF]),
+                .rearrange("p g (l b) -> p (g l) b", b=B)
+                .unsqueeze(2)
+                .to_broadcast([P, 2 * L, Q, B]),
             )
             nc.vector.tensor_copy(
-                out=xes[:, :, 2 * b : 2 * b + 2].bitcast(I32),
-                in_=xs[:, :, L * b : L * b + L]
+                out=xes[:].rearrange("p g l m b -> p (g l) (m b)").bitcast(I32),
+                in_=xs[:]
                 .bitcast(I32)
-                .rearrange("p g (s m) -> p g s m", m=HALF // 4)
-                .unsqueeze(3)
-                .to_broadcast([P, 2, 2, HALF, HALF // 4]),
+                .rearrange("p g l -> p (g l)")
+                .unsqueeze(2)
+                .to_broadcast([P, 2 * L, Q]),
             )
 
-        def product(b, blk):
-            i_half, j_half = BLOCKS[blk]
-            pr = prod.tile([P, 2, HALF, HALF, 4], BF16, align_bytes=64, name="pr", tag="pr")
-            t_major = L * b + HALF * i_half
-            t_minor = L * b + HALF * j_half
+        def product(blk):
+            i, j = BLOCKS[blk]
+            pr = prod.tile([P, 2, Q, Q, B * 4], BF16, align_bytes=64, name="pr", tag="pr")
             for g in range(2):
                 nc.vector.tensor_tensor(
                     out=pr[:, g],
-                    in0=xg[:, g, t_major : t_major + HALF, :]
-                    .unsqueeze(2)
-                    .to_broadcast([P, HALF, HALF, 4]),
-                    in1=xg[:, g, t_minor : t_minor + HALF, :]
-                    .unsqueeze(1)
-                    .to_broadcast([P, HALF, HALF, 4]),
+                    in0=xg[:, g, Q * i : Q * i + Q, :].unsqueeze(2).to_broadcast([P, Q, Q, B * 4]),
+                    in1=xg[:, g, Q * j : Q * j + Q, :].unsqueeze(1).to_broadcast([P, Q, Q, B * 4]),
                     op=ALU.mult,
                 )
             nc.vector.quantize_mx(
-                out=pc[:, 3 * b + blk].rearrange("p g c -> p (g c)").bitcast(FP8X4),
-                scales=ps[:, 3 * b + blk].rearrange("p g c -> p (g c)"),
-                in_=pr[:].rearrange("p g a m t -> p (g a m t)"),
+                out=pc[:, blk].rearrange("p g c -> p (g c)").bitcast(FP8X4),
+                scales=ps[:, blk].rearrange("p g c -> p (g c)"),
+                in_=pr[:].rearrange("p g a m k -> p (g a m k)"),
             )
 
         def tables(gh):
-            for table, m in ((tab_a, 1), (tab_c, 2)):
+            for table, m in ((tab_c, 2), (tab_a, 1)):
                 tp = psum.tile([P, 4, P], F32, name="tp", tag="u")
                 for t in range(4):
                     h0 = 512 * gh + P * t
@@ -176,9 +173,9 @@ def tile_srlbertold_pa_kernel(tc, seq_out, W_proj, b_proj, W_out, b_out, out):
                     )
             if gh not in OWN_GROUP:
                 nc.vector.tensor_tensor(
-                    out=tab_d[:, 4 * gh : 4 * gh + 4, :],
-                    in0=tab_a[:, 4 * gh : 4 * gh + 4, :],
-                    in1=tab_c[:, 4 * gh : 4 * gh + 4, :],
+                    out=tab_e[:, gh],
+                    in0=tab_c[:, 4 * gh : 4 * gh + 4, :].rearrange("p (q u) k -> p q k u", u=2),
+                    in1=tab_a[:, 4 * gh : 4 * gh + 4, :].rearrange("p (q u) k -> p q k u", u=2),
                     op=ALU.subtract,
                 )
 
@@ -190,16 +187,12 @@ def tile_srlbertold_pa_kernel(tc, seq_out, W_proj, b_proj, W_out, b_out, out):
                 in_=grp_o[:].rearrange("p g n t -> p (g n t)"),
             )
 
-        def of_major(table, plane, token):
-            view = table[:, plane : plane + 2, token : token + HALF].rearrange("p u a -> p a u")
-            return view.unsqueeze(2).to_broadcast([P, HALF, HALF, 2])
+        def of_minor(table, plane, j):
+            view = table[:, plane : plane + 2, Q * B * j : Q * B * (j + 1)].rearrange("p u k -> p k u")
+            return view.unsqueeze(1).to_broadcast([P, Q, Q * B, 2])
 
-        def of_minor(table, plane, token):
-            view = table[:, plane : plane + 2, token : token + HALF].rearrange("p u m -> p m u")
-            return view.unsqueeze(1).to_broadcast([P, HALF, HALF, 2])
-
-        def pair_sums(b, blk, gh, m_in):
-            slot = 2 * b + BLOCKS[blk][1]
+        def pair_sums(blk, gh, m_in):
+            i = BLOCKS[blk][0]
             banks = []
             for q in range(2):
                 bank = psum.tile([P, 2, COLS], F32, name="bank", tag="u")
@@ -210,8 +203,8 @@ def tile_srlbertold_pa_kernel(tc, seq_out, W_proj, b_proj, W_out, b_out, out):
                             out=bank[:, u, :],
                             lhsT=wc[0][:, g, h0 : h0 + P].bitcast(FP8X4),
                             lhsT_scale=ws[0][:, g, h0 : h0 + P],
-                            rhs=pc[:, 3 * b + blk, g, :].bitcast(FP8X4),
-                            rhs_scale=ps[:, 3 * b + blk, g, :],
+                            rhs=pc[:, blk, g, :].bitcast(FP8X4),
+                            rhs_scale=ps[:, blk, g, :],
                             start=(g == 0),
                             stop=False,
                         )
@@ -220,8 +213,8 @@ def tile_srlbertold_pa_kernel(tc, seq_out, W_proj, b_proj, W_out, b_out, out):
                             out=bank[:, u, :],
                             lhsT=wc[m_in][:, g, h0 : h0 + P].bitcast(FP8X4),
                             lhsT_scale=ws[m_in][:, g, h0 : h0 + P],
-                            rhs=xec[:, g, slot].rearrange("p a m -> p (a m)").bitcast(FP8X4),
-                            rhs_scale=xes[:, g, slot].rearrange("p a m -> p (a m)"),
+                            rhs=xec[:, g, Q * i : Q * i + Q].rearrange("p a m b -> p (a m b)").bitcast(FP8X4),
+                            rhs_scale=xes[:, g, Q * i : Q * i + Q].rearrange("p a m b -> p (a m b)"),
                             start=False,
                             stop=(g == 1),
                         )
@@ -232,8 +225,8 @@ def tile_srlbertold_pa_kernel(tc, seq_out, W_proj, b_proj, W_out, b_out, out):
             z = zpool.tile([P, 2, COLS, 2], F32, name="z", tag="z")
             for q in range(2):
                 nc.vector.tensor_tensor(
-                    out=z[:, q].rearrange("p (a m) u -> p a m u", m=HALF),
-                    in0=banks[q][:].rearrange("p u (a m) -> p a m u", m=HALF),
+                    out=z[:, q].rearrange("p (a k) u -> p a k u", a=Q),
+                    in0=banks[q][:].rearrange("p u (a k) -> p a k u", a=Q),
                     in1=addends[q],
                     op=ALU.add,
                 )
@@ -249,31 +242,33 @@ def tile_srlbertold_pa_kernel(tc, seq_out, W_proj, b_proj, W_out, b_out, out):
                 in_=pj[:].rearrange("p c t -> p (c t)"),
             )
 
-        def unit(b, blk, gh):
-            i_half, j_half = BLOCKS[blk]
-            t_major = L * b + HALF * i_half
-            t_minor = L * b + HALF * j_half
+        def unit(tau, blk, mirrored, gh, banks):
+            i, j = BLOCKS[blk]
             planes = (4 * gh, 4 * gh + 2)
-            banks = pair_sums(b, blk, gh, 2)
-            squash(banks, [of_major(tab_a, pl, t_major) for pl in planes], 4 * b + (0, 1, 3)[blk], gh)
-            if blk != 1:
-                return
-            if gh in OWN_GROUP:
-                banks = pair_sums(b, blk, gh, 1)
-                squash(banks, [of_major(tab_c, pl, t_major) for pl in planes], 4 * b + 2, gh)
+            if not mirrored:
+                banks = pair_sums(blk, gh, 1)
+                squash(banks, [of_minor(tab_c, pl, j) for pl in planes], tau, gh)
+            elif gh in OWN_GROUP:
+                banks = pair_sums(blk, gh, 2)
+                squash(banks, [of_minor(tab_a, pl, j) for pl in planes], tau, gh)
             else:
                 s2 = spool.tile([P, 2, COLS, 2], F32, name="s2", tag="s2")
-                views = [s2[:, q].rearrange("p (a m) u -> p a m u", m=HALF) for q in range(2)]
                 for q in range(2):
                     nc.vector.tensor_tensor(
-                        out=views[q],
-                        in0=of_major(tab_c, planes[q], t_major),
-                        in1=of_minor(tab_d, planes[q], t_minor),
+                        out=s2[:, q].rearrange("p (a m b) u -> p a m b u", a=Q, m=Q),
+                        in0=tab_e[:, gh, q, Q * B * i : Q * B * (i + 1), :]
+                        .rearrange("p (a b) u -> p a b u", b=B)
+                        .unsqueeze(2)
+                        .to_broadcast([P, Q, Q, B, 2]),
+                        in1=of_minor(tab_a, planes[q], j)
+                        .rearrange("p a (m b) u -> p a m b u", b=B),
                         op=ALU.add,
                     )
-                squash(banks, views, 4 * b + 2, gh)
+                squash(banks, [s2[:, q].rearrange("p (a k) u -> p a k u", a=Q) for q in range(2)], tau, gh)
+            return banks
 
-        def labels(tau, o_sb):
+        def labels(tau, blk, mirrored):
+            i, j = BLOCKS[blk]
             ob = psum_o.tile([P, COLS], F32, name="ob", tag="o")
             for gh in range(2):
                 nc.tensor.matmul_mx(
@@ -285,15 +280,14 @@ def tile_srlbertold_pa_kernel(tc, seq_out, W_proj, b_proj, W_out, b_out, out):
                     start=(gh == 0),
                     stop=(gh == 1),
                 )
-            kind = tau % 4
-            row0 = HALF * (kind // 2)
-            col0 = HALF * (kind % 2)
-            if kind == 2:
-                src = ob[:].rearrange("p (a m) -> p m a", m=HALF)
+            if mirrored:
+                src = ob[:].rearrange("p (a m b) -> p b m a", a=Q, m=Q)
+                row0, col0 = Q * j, Q * i
             else:
-                src = ob[:].rearrange("p (a m) -> p a m", m=HALF)
+                src = ob[:].rearrange("p (a m b) -> p b a m", a=Q, m=Q)
+                row0, col0 = Q * i, Q * j
             nc.scalar.activation(
-                out=o_sb[:, row0 : row0 + HALF, col0 : col0 + HALF],
+                out=o_sb[:, :, row0 : row0 + Q, col0 : col0 + Q],
                 in_=src,
                 func=ACTF.Identity,
                 bias=bias[:, 8:9],
@@ -303,46 +297,49 @@ def tile_srlbertold_pa_kernel(tc, seq_out, W_proj, b_proj, W_out, b_out, out):
         pack_piece(raws[0], *first[0], on_vector=True)
         quantise_x()
         pack_piece(raws[1], *first[1], on_vector=False)
-        product(0, 0)
+        product(0)
         pack_piece(raws[2], *first[2], on_vector=True)
+        expand_x()
         pack_piece(raws[3], *first[3], on_vector=False)
-        expand_x(0)
         pack_piece(raws[4], *first[4], on_vector=False)
         pack_piece(raws[5], *first[5], on_vector=False)
         raws2 = [load_piece(m, c, g) for (m, c, g) in second]
         nc.sync.dma_start(out=raw_o[:], in_=W_out.rearrange("(a p) n -> p a n", p=P))
         tables(0)
 
-        order = [(b, blk, 0) for b in range(2) for blk in range(3)]
-        order += [(b, blk, 1) for b in range(2) for blk in range(3)]
-        order += [(b, blk, gh) for b in range(2, 4) for blk in range(3) for gh in range(2)]
+        taus = {}
+        for blk, (i, j) in enumerate(BLOCKS):
+            taus[(blk, False)] = len(taus)
+            if i != j:
+                taus[(blk, True)] = len(taus)
 
-        made = set([(0, 0)])
-        expanded = set([0])
-        o_tiles = {}
-        for n, (b, blk, gh) in enumerate(order):
-            for b2, blk2, gh2 in order[n : n + 3]:
-                if (b2, blk2) not in made:
-                    product(b2, blk2)
-                    made.add((b2, blk2))
-                if b2 not in expanded:
-                    expand_x(b2)
-                    expanded.add(b2)
-            unit(b, blk, gh)
+        def tiles(blks, gh):
+            return [(blk, mir, gh) for blk in blks for mir in (False, True) if (blk, mir) in taus]
+
+        early = range(4)
+        order = tiles(early, 0) + tiles(early, 1)
+        for blk in range(4, 10):
+            order += tiles([blk], 0) + tiles([blk], 1)
+
+        made = set([0])
+        kept_banks = None
+        for n, (blk, mir, gh) in enumerate(order):
+            for blk2, mir2, gh2 in order[n : n + 3]:
+                if blk2 not in made:
+                    product(blk2)
+                    made.add(blk2)
+            kept_banks = unit(taus[(blk, mir)], blk, mir, gh, kept_banks)
             if n == 0:
                 for k, (m, c, g) in enumerate(second):
                     pack_piece(raws2[k], m, c, g, on_vector=False)
                 pack_w_out()
-            if n == 4:
+            if n == 5:
                 tables(1)
             if gh == 1:
-                if b not in o_tiles:
-                    o_tiles[b] = opool.tile([P, L, L], F32, name="o_sb", tag="o_sb")
-                for tau in ((0,), (1, 2), (3,))[blk]:
-                    labels(4 * b + tau, o_tiles[b])
-                if blk >= 1:
-                    r0 = HALF * (blk // 2)
+                labels(taus[(blk, mir)], blk, mir)
+                i, j = BLOCKS[blk]
+                if j == 3 and (mir or i == 3):
                     nc.sync.dma_start(
-                        out=out[b, :, r0 : r0 + HALF, :].rearrange("k i j -> k (i j)"),
-                        in_=o_tiles[b][:, r0 : r0 + HALF, :].rearrange("p i j -> p (i j)"),
+                        out=out[:, :, Q * i : Q * i + Q, :].rearrange("b k i j -> k b (i j)"),
+                        in_=o_sb[:, :, Q * i : Q * i + Q, :].rearrange("p b i j -> p b (i j)"),
                     )

@@ -113,23 +113,23 @@ def tile_srlbertold_pa_kernel(tc, seq_out, W_proj, b_proj, W_out, b_out, out):
                 in_=xg[:].rearrange("p g l k -> p (g l k)"),
             )
 
-        def expand_x():
-            nc.vector.tensor_copy(
-                out=xec[:].bitcast(I32).rearrange("p g l m b -> p (g l) m b"),
-                in_=xc[:]
-                .bitcast(I32)
-                .rearrange("p g (l b) -> p (g l) b", b=B)
-                .unsqueeze(2)
-                .to_broadcast([P, 2 * L, Q, B]),
-            )
-            nc.vector.tensor_copy(
-                out=xes[:].rearrange("p g l m b -> p (g l) (m b)").bitcast(I32),
-                in_=xs[:]
-                .bitcast(I32)
-                .rearrange("p g l -> p (g l)")
-                .unsqueeze(2)
-                .to_broadcast([P, 2 * L, Q]),
-            )
+        def expand_x(engine, i, k):
+            for g in range(2):
+                engine.tensor_copy(
+                    out=xec[:, g, Q * i : Q * k].bitcast(I32),
+                    in_=xc[:, g, Q * B * i : Q * B * k]
+                    .bitcast(I32)
+                    .rearrange("p (l b) -> p l b", b=B)
+                    .unsqueeze(2)
+                    .to_broadcast([P, Q * (k - i), Q, B]),
+                )
+                engine.tensor_copy(
+                    out=xes[:, g, Q * i : Q * k].rearrange("p l m b -> p l (m b)").bitcast(I32),
+                    in_=xs[:, g, Q * B * i : Q * B * k]
+                    .bitcast(I32)
+                    .unsqueeze(2)
+                    .to_broadcast([P, Q * (k - i), Q]),
+                )
 
         def product(blk):
             i, j = BLOCKS[blk]
@@ -242,14 +242,19 @@ def tile_srlbertold_pa_kernel(tc, seq_out, W_proj, b_proj, W_out, b_out, out):
                 in_=pj[:].rearrange("p c t -> p (c t)"),
             )
 
+        def sums(blk, mirrored, gh):
+            if not mirrored:
+                return pair_sums(blk, gh, 1)
+            if gh in OWN_GROUP:
+                return pair_sums(blk, gh, 2)
+            return None
+
         def unit(tau, blk, mirrored, gh, banks):
             i, j = BLOCKS[blk]
             planes = (4 * gh, 4 * gh + 2)
             if not mirrored:
-                banks = pair_sums(blk, gh, 1)
                 squash(banks, [of_minor(tab_c, pl, j) for pl in planes], tau, gh)
             elif gh in OWN_GROUP:
-                banks = pair_sums(blk, gh, 2)
                 squash(banks, [of_minor(tab_a, pl, j) for pl in planes], tau, gh)
             else:
                 s2 = spool.tile([P, 2, COLS, 2], F32, name="s2", tag="s2")
@@ -265,7 +270,6 @@ def tile_srlbertold_pa_kernel(tc, seq_out, W_proj, b_proj, W_out, b_out, out):
                         op=ALU.add,
                     )
                 squash(banks, [s2[:, q].rearrange("p (a k) u -> p a k u", a=Q) for q in range(2)], tau, gh)
-            return banks
 
         def labels(tau, blk, mirrored):
             i, j = BLOCKS[blk]
@@ -294,19 +298,6 @@ def tile_srlbertold_pa_kernel(tc, seq_out, W_proj, b_proj, W_out, b_out, out):
                 scale=1.0,
             )
 
-        pack_piece(raws[0], *first[0], on_vector=True)
-        quantise_x()
-        pack_piece(raws[1], *first[1], on_vector=False)
-        product(0)
-        pack_piece(raws[2], *first[2], on_vector=True)
-        expand_x()
-        pack_piece(raws[3], *first[3], on_vector=False)
-        pack_piece(raws[4], *first[4], on_vector=False)
-        pack_piece(raws[5], *first[5], on_vector=False)
-        raws2 = [load_piece(m, c, g) for (m, c, g) in second]
-        nc.sync.dma_start(out=raw_o[:], in_=W_out.rearrange("(a p) n -> p a n", p=P))
-        tables(0)
-
         taus = {}
         for blk, (i, j) in enumerate(BLOCKS):
             taus[(blk, False)] = len(taus)
@@ -321,14 +312,33 @@ def tile_srlbertold_pa_kernel(tc, seq_out, W_proj, b_proj, W_out, b_out, out):
         for blk in range(4, 10):
             order += tiles([blk], 0) + tiles([blk], 1)
 
-        made = set([0])
-        kept_banks = None
+        pack_piece(raws[0], *first[0], on_vector=True)
+        quantise_x()
+        pack_piece(raws[1], *first[1], on_vector=False)
+        product(0)
+        expand_x(nc.vector, 0, 1)
+        expand_x(nc.gpsimd, 1, 4)
+        pack_piece(raws[2], *first[2], on_vector=True)
+        pack_piece(raws[3], *first[3], on_vector=False)
+        product(1)
+        banks_of = {}
+        for n in range(2):
+            banks_of[n] = sums(*order[n])
+        pack_piece(raws[4], *first[4], on_vector=False)
+        pack_piece(raws[5], *first[5], on_vector=False)
+        raws2 = [load_piece(m, c, g) for (m, c, g) in second]
+        nc.sync.dma_start(out=raw_o[:], in_=W_out.rearrange("(a p) n -> p a n", p=P))
+        tables(0)
+
+        made = set([0, 1])
         for n, (blk, mir, gh) in enumerate(order):
             for blk2, mir2, gh2 in order[n : n + 3]:
                 if blk2 not in made:
                     product(blk2)
                     made.add(blk2)
-            kept_banks = unit(taus[(blk, mir)], blk, mir, gh, kept_banks)
+            if n not in banks_of:
+                banks_of[n] = sums(blk, mir, gh) or banks_of[n - 1]
+            unit(taus[(blk, mir)], blk, mir, gh, banks_of[n])
             if n == 0:
                 for k, (m, c, g) in enumerate(second):
                     pack_piece(raws2[k], m, c, g, on_vector=False)

@@ -22,7 +22,7 @@ COLS = Q * Q * B
 FLOPS = 2 * B * L * L * H * H + 2 * 2 * B * L * H * H + 2 * B * L * L * H * P
 
 BLOCKS = [(i, j) for i in range(4) for j in range(i, 4)]
-OWN_GROUP = (0,)
+DERIVED = [(blk, 1) for blk in (1, 3, 5, 6, 8)]
 
 
 def tile_srlbertold_pa_kernel(tc, seq_out, W_proj, b_proj, W_out, b_out, out):
@@ -64,8 +64,8 @@ def tile_srlbertold_pa_kernel(tc, seq_out, W_proj, b_proj, W_out, b_out, out):
 
         make_identity(nc, ident[:])
         nc.sync.dma_start(out=x_sb[:], in_=seq_out.flatten_outer_dims())
-        nc.vector.memset(bias_rows[:], 0.0)
-        nc.vector.memset(xs[:].bitcast(I32), 0)
+        nc.gpsimd.memset(bias_rows[:], 0.0)
+        nc.gpsimd.memset(xs[:].bitcast(I32), 0)
         nc.scalar.dma_start(out=bias_rows[0:8, :], in_=b_proj.rearrange("(r c) -> r c", c=P))
         nc.scalar.dma_start(out=bias_rows[8:9, :], in_=b_out.rearrange("(r c) -> r c", c=P))
 
@@ -75,19 +75,30 @@ def tile_srlbertold_pa_kernel(tc, seq_out, W_proj, b_proj, W_out, b_out, out):
             nc.sync.dma_start(out=raw[:], in_=rows.rearrange("(t p) n -> p t n", p=P))
             return raw
 
-        def pack_piece(raw, m, c, g, on_vector):
-            grp = wgrp.tile([P, 512, 4], BF16, align_bytes=64, name="grp", tag="grp")
-            dst = grp[:].rearrange("p (c i) t -> p c t i", i=4)
-            src = raw[:].rearrange("p t (c i) -> p c t i", i=4)
+        def pack_half(raw, grp, piece, half, on_vector):
+            m, c, g = piece
+            cols = slice(256 * half, 256 * half + 256)
+            dst = grp[:, cols, :].rearrange("p (c i) t -> p c t i", i=4)
+            src = raw[:, :, cols].rearrange("p t (c i) -> p c t i", i=4)
             if on_vector:
                 nc.vector.tensor_copy(out=dst, in_=src)
             else:
                 nc.scalar.copy(out=dst, in_=src)
+            col0 = 512 * c + 256 * half
             nc.vector.quantize_mx(
-                out=wc[m][:, g, 512 * c : 512 * c + 512].bitcast(FP8X4),
-                scales=ws[m][:, g, 512 * c : 512 * c + 512],
-                in_=grp[:].rearrange("p n t -> p (n t)"),
+                out=wc[m][:, g, col0 : col0 + 256].bitcast(FP8X4),
+                scales=ws[m][:, g, col0 : col0 + 256],
+                in_=grp[:, cols, :].rearrange("p n t -> p (n t)"),
             )
+
+        def group_tile():
+            grp = wgrp.tile([P, 512, 4], BF16, align_bytes=64, name="grp", tag="grp")
+            return grp
+
+        def pack_piece(raw, m, c, g, on_vector):
+            grp = group_tile()
+            for half in range(2):
+                pack_half(raw, grp, (m, c, g), half, on_vector)
 
         first = [(0, 0, 0), (0, 0, 1), (1, 0, 0), (1, 0, 1), (2, 0, 0), (2, 0, 1)]
         second = [(0, 1, 0), (0, 1, 1), (1, 1, 0), (1, 1, 1), (2, 1, 0), (2, 1, 1)]
@@ -149,7 +160,7 @@ def tile_srlbertold_pa_kernel(tc, seq_out, W_proj, b_proj, W_out, b_out, out):
 
         def tables(gh):
             for table, m in ((tab_c, 2), (tab_a, 1)):
-                tp = psum.tile([P, 4, P], F32, name="tp", tag="u")
+                tp = psum_o.tile([P, 4, P], F32, name="tp", tag="o")
                 for t in range(4):
                     h0 = 512 * gh + P * t
                     for g in range(2):
@@ -171,7 +182,7 @@ def tile_srlbertold_pa_kernel(tc, seq_out, W_proj, b_proj, W_out, b_out, out):
                         bias=bias[:, plane : plane + 1],
                         scale=1.0,
                     )
-            if gh not in OWN_GROUP:
+            if any(gh == half for (blk, half) in DERIVED):
                 nc.vector.tensor_tensor(
                     out=tab_e[:, gh],
                     in0=tab_c[:, 4 * gh : 4 * gh + 4, :].rearrange("p (q u) k -> p q k u", u=2),
@@ -187,9 +198,9 @@ def tile_srlbertold_pa_kernel(tc, seq_out, W_proj, b_proj, W_out, b_out, out):
                 in_=grp_o[:].rearrange("p g n t -> p (g n t)"),
             )
 
-        def of_minor(table, plane, j):
+        def of_minor(table, plane, j, majors=Q):
             view = table[:, plane : plane + 2, Q * B * j : Q * B * (j + 1)].rearrange("p u k -> p k u")
-            return view.unsqueeze(1).to_broadcast([P, Q, Q * B, 2])
+            return view.unsqueeze(1).to_broadcast([P, majors, Q * B, 2])
 
         def pair_sums(blk, gh, m_in):
             i = BLOCKS[blk][0]
@@ -221,42 +232,42 @@ def tile_srlbertold_pa_kernel(tc, seq_out, W_proj, b_proj, W_out, b_out, out):
                 banks.append(bank)
             return banks
 
-        def squash(banks, addends, tau, gh):
+        def squash(banks, addend, tau, gh, splits):
+            majors = Q // splits
+            groups = [slice(COLS // splits * s, COLS // splits * (s + 1)) for s in range(splits)]
             z = zpool.tile([P, 2, COLS, 2], F32, name="z", tag="z")
-            for q in range(2):
-                nc.vector.tensor_tensor(
-                    out=z[:, q].rearrange("p (a k) u -> p a k u", a=Q),
-                    in0=banks[q][:].rearrange("p u (a k) -> p a k u", a=Q),
-                    in1=addends[q],
-                    op=ALU.add,
-                )
             pj = jpool.tile([P, COLS, 4], BF16, align_bytes=64, name="pj", tag="pj")
-            nc.scalar.activation(
-                out=pj[:].rearrange("p c (q u) -> p c q u", u=2),
-                in_=z[:].rearrange("p q c u -> p c q u"),
-                func=ACTF.Tanh,
-            )
-            nc.vector.quantize_mx(
-                out=jc[:, tau, gh, :].bitcast(FP8X4),
-                scales=js[:, tau, gh, :],
-                in_=pj[:].rearrange("p c t -> p (c t)"),
-            )
+            for q in range(2):
+                for cols in groups:
+                    nc.vector.tensor_tensor(
+                        out=z[:, q, cols, :].rearrange("p (a k) u -> p a k u", a=majors),
+                        in0=banks[q][:, :, cols].rearrange("p u (a k) -> p a k u", a=majors),
+                        in1=addend(q, majors, cols),
+                        op=ALU.add,
+                    )
+                    if q == 1:
+                        nc.scalar.activation(
+                            out=pj[:, cols, :].rearrange("p c (q u) -> p c q u", u=2),
+                            in_=z[:, :, cols, :].rearrange("p q c u -> p c q u"),
+                            func=ACTF.Tanh,
+                        )
+            for cols in groups:
+                nc.vector.quantize_mx(
+                    out=jc[:, tau, gh, cols].bitcast(FP8X4),
+                    scales=js[:, tau, gh, cols],
+                    in_=pj[:, cols, :].rearrange("p c t -> p (c t)"),
+                )
 
         def sums(blk, mirrored, gh):
             if not mirrored:
                 return pair_sums(blk, gh, 1)
-            if gh in OWN_GROUP:
+            if (blk, gh) not in DERIVED:
                 return pair_sums(blk, gh, 2)
             return None
 
-        def unit(tau, blk, mirrored, gh, banks):
+        def unit(tau, blk, mirrored, gh, banks, splits):
             i, j = BLOCKS[blk]
-            planes = (4 * gh, 4 * gh + 2)
-            if not mirrored:
-                squash(banks, [of_minor(tab_c, pl, j) for pl in planes], tau, gh)
-            elif gh in OWN_GROUP:
-                squash(banks, [of_minor(tab_a, pl, j) for pl in planes], tau, gh)
-            else:
+            if mirrored and (blk, gh) in DERIVED:
                 s2 = spool.tile([P, 2, COLS, 2], F32, name="s2", tag="s2")
                 for q in range(2):
                     nc.vector.tensor_tensor(
@@ -265,38 +276,58 @@ def tile_srlbertold_pa_kernel(tc, seq_out, W_proj, b_proj, W_out, b_out, out):
                         .rearrange("p (a b) u -> p a b u", b=B)
                         .unsqueeze(2)
                         .to_broadcast([P, Q, Q, B, 2]),
-                        in1=of_minor(tab_a, planes[q], j)
+                        in1=of_minor(tab_a, 4 * gh + 2 * q, j)
                         .rearrange("p a (m b) u -> p a m b u", b=B),
                         op=ALU.add,
                     )
-                squash(banks, [s2[:, q].rearrange("p (a k) u -> p a k u", a=Q) for q in range(2)], tau, gh)
 
-        def labels(tau, blk, mirrored):
-            i, j = BLOCKS[blk]
-            ob = psum_o.tile([P, COLS], F32, name="ob", tag="o")
-            for gh in range(2):
-                nc.tensor.matmul_mx(
-                    out=ob[:],
-                    lhsT=oc[:, gh, :].bitcast(FP8X4),
-                    lhsT_scale=os_[:, gh, :],
-                    rhs=jc[:, tau, gh, :].bitcast(FP8X4),
-                    rhs_scale=js[:, tau, gh, :],
-                    start=(gh == 0),
-                    stop=(gh == 1),
-                )
-            if mirrored:
-                src = ob[:].rearrange("p (a m b) -> p b m a", a=Q, m=Q)
-                row0, col0 = Q * j, Q * i
+                def addend(q, majors, cols):
+                    return s2[:, q, cols, :].rearrange("p (a k) u -> p a k u", a=majors)
+
             else:
-                src = ob[:].rearrange("p (a m b) -> p b a m", a=Q, m=Q)
-                row0, col0 = Q * i, Q * j
-            nc.scalar.activation(
-                out=o_sb[:, :, row0 : row0 + Q, col0 : col0 + Q],
-                in_=src,
-                func=ACTF.Identity,
-                bias=bias[:, 8:9],
-                scale=1.0,
-            )
+                table = tab_a if mirrored else tab_c
+
+                def addend(q, majors, cols):
+                    return of_minor(table, 4 * gh + 2 * q, j, majors)
+
+            squash(banks, addend, tau, gh, splits)
+
+        def labels(tau, blk, mirrored, splits):
+            i, j = BLOCKS[blk]
+            width = COLS // splits
+            for s in range(splits):
+                ob = psum_o.tile([P, COLS], F32, name="ob", tag="o")
+                cols = slice(width * s, width * (s + 1))
+                for gh in range(2):
+                    nc.tensor.matmul_mx(
+                        out=ob[:, 0:width],
+                        lhsT=oc[:, gh, :].bitcast(FP8X4),
+                        lhsT_scale=os_[:, gh, :],
+                        rhs=jc[:, tau, gh, cols].bitcast(FP8X4),
+                        rhs_scale=js[:, tau, gh, cols],
+                        start=(gh == 0),
+                        stop=(gh == 1),
+                    )
+                rows = Q // splits
+                if mirrored:
+                    src = ob[:].rearrange("p (a m b) -> p b m a", a=Q, m=Q)
+                    dst = o_sb[:, :, Q * j : Q * j + Q, Q * i : Q * i + Q]
+                else:
+                    src = ob[:, 0:width].rearrange("p (a m b) -> p b a m", a=rows, m=Q)
+                    dst = o_sb[:, :, Q * i + rows * s : Q * i + rows * (s + 1), Q * j : Q * j + Q]
+                nc.scalar.activation(
+                    out=dst,
+                    in_=src,
+                    func=ACTF.Identity,
+                    bias=bias[:, 8:9],
+                    scale=1.0,
+                )
+                if j == 3 and not mirrored:
+                    row0 = Q * i + rows * s
+                    nc.sync.dma_start(
+                        out=out[:, :, row0 : row0 + rows, :].rearrange("b k i j -> k b (i j)"),
+                        in_=o_sb[:, :, row0 : row0 + rows, :].rearrange("p b i j -> p b (i j)"),
+                    )
 
         taus = {}
         for blk, (i, j) in enumerate(BLOCKS):
@@ -307,9 +338,9 @@ def tile_srlbertold_pa_kernel(tc, seq_out, W_proj, b_proj, W_out, b_out, out):
         def tiles(blks, gh):
             return [(blk, mir, gh) for blk in blks for mir in (False, True) if (blk, mir) in taus]
 
-        early = range(4)
+        early = range(6)
         order = tiles(early, 0) + tiles(early, 1)
-        for blk in range(4, 10):
+        for blk in range(6, 10):
             order += tiles([blk], 0) + tiles([blk], 1)
 
         pack_piece(raws[0], *first[0], on_vector=True)
@@ -318,7 +349,7 @@ def tile_srlbertold_pa_kernel(tc, seq_out, W_proj, b_proj, W_out, b_out, out):
         product(0)
         expand_x(nc.vector, 0, 1)
         expand_x(nc.gpsimd, 1, 4)
-        pack_piece(raws[2], *first[2], on_vector=True)
+        pack_piece(raws[2], *first[2], on_vector=False)
         pack_piece(raws[3], *first[3], on_vector=False)
         product(1)
         banks_of = {}
@@ -331,6 +362,8 @@ def tile_srlbertold_pa_kernel(tc, seq_out, W_proj, b_proj, W_out, b_out, out):
         tables(0)
 
         made = set([0, 1])
+        grps = {}
+        halves_done = 0
         for n, (blk, mir, gh) in enumerate(order):
             for blk2, mir2, gh2 in order[n : n + 3]:
                 if blk2 not in made:
@@ -338,18 +371,16 @@ def tile_srlbertold_pa_kernel(tc, seq_out, W_proj, b_proj, W_out, b_out, out):
                     made.add(blk2)
             if n not in banks_of:
                 banks_of[n] = sums(blk, mir, gh) or banks_of[n - 1]
-            unit(taus[(blk, mir)], blk, mir, gh, banks_of[n])
-            if n == 0:
-                for k, (m, c, g) in enumerate(second):
-                    pack_piece(raws2[k], m, c, g, on_vector=False)
-                pack_w_out()
-            if n == 5:
+            splits = 2 if n == len(order) - 1 else 1
+            unit(taus[(blk, mir)], blk, mir, gh, banks_of[n], splits)
+            while halves_done < min(12, 4 * (n + 1) // 3):
+                k, half = divmod(halves_done, 2)
+                if half == 0:
+                    grps[k] = group_tile()
+                pack_half(raws2[k], grps[k], second[k], half, on_vector=False)
+                halves_done += 1
+            if n == 8:
                 tables(1)
+                pack_w_out()
             if gh == 1:
-                labels(taus[(blk, mir)], blk, mir)
-                i, j = BLOCKS[blk]
-                if j == 3 and (mir or i == 3):
-                    nc.sync.dma_start(
-                        out=out[:, :, Q * i : Q * i + Q, :].rearrange("b k i j -> k b (i j)"),
-                        in_=o_sb[:, :, Q * i : Q * i + Q, :].rearrange("p b i j -> p b (i j)"),
-                    )
+                labels(taus[(blk, mir)], blk, mir, splits)

from contextlib import ExitStack

import concourse.mybir as mybir
from concourse.masks import make_identity

FP8X4 = mybir.dt.float8_e4m3fn_x4
BF16 = mybir.dt.bfloat16
F32 = mybir.dt.float32
U32 = mybir.dt.uint32
U8 = mybir.dt.uint8
I32 = mybir.dt.int32
ACTF = mybir.ActivationFunctionType
ALU = mybir.AluOpType

P = 128
B = 4
L = 32
H = 1024
Q = 8
COLS = Q * Q * B

FLOPS = 2 * B * L * L * H * H + 2 * 2 * B * L * H * H + 2 * B * L * L * H * P

BLOCKS = [(i, j) for i in range(4) for j in range(i, 4)]
DERIVED = [(blk, 1) for blk in (1, 3, 5, 6, 8)]


def tile_srlbertold_pa_kernel(tc, seq_out, W_proj, b_proj, W_out, b_out, out):
    nc = tc.nc
    with ExitStack() as ctx:
        keep = ctx.enter_context(tc.tile_pool(name="keep", bufs=1))
        wraw = ctx.enter_context(tc.tile_pool(name="wraw", bufs=6))
        wgrp = ctx.enter_context(tc.tile_pool(name="wgrp", bufs=3))
        prod = ctx.enter_context(tc.tile_pool(name="prod", bufs=3))
        zpool = ctx.enter_context(tc.tile_pool(name="zpool", bufs=3))
        spool = ctx.enter_context(tc.tile_pool(name="spool", bufs=2))
        jpool = ctx.enter_context(tc.tile_pool(name="jpool", bufs=3))
        psum = ctx.enter_context(tc.psum_pool(name="psum", bufs=6))
        psum_o = ctx.enter_context(tc.psum_pool(name="psum_o", bufs=2))

        ident = keep.tile([P, P], BF16)
        x_sb = keep.tile([P, H], BF16)
        bias_rows = keep.tile([P, P], BF16)
        bias = keep.tile([P, 16], F32)
        xg = keep.tile([P, 2, L, B * 4], BF16, align_bytes=64)
        xc = keep.tile([P, 2, P], U32, align_bytes=64)
        xs = keep.tile([P, 2, P], U8, align_bytes=64)
        xec = keep.tile([P, 2, L, Q, B], U32, align_bytes=64)
        xes = keep.tile([P, 2, L, Q, B], U8, align_bytes=64)
        wc = [keep.tile([P, 2, H], U32, align_bytes=64, name="wc%d" % m) for m in range(3)]
        ws = [keep.tile([P, 2, H], U8, align_bytes=64, name="ws%d" % m) for m in range(3)]
        raw_o = keep.tile([P, 8, P], BF16)
        grp_o = keep.tile([P, 2, P, 4], BF16, align_bytes=64)
        oc = keep.tile([P, 2, P], U32, align_bytes=64)
        os_ = keep.tile([P, 2, P], U8, align_bytes=64)
        tab_a = keep.tile([P, 8, P], F32)
        tab_c = keep.tile([P, 8, P], F32)
        tab_e = keep.tile([P, 2, 2, P, 2], F32)
        pc = keep.tile([P, 10, 2, COLS], U32, align_bytes=64)
        ps = keep.tile([P, 10, 2, COLS], U8, align_bytes=64)
        jc = keep.tile([P, 16, 2, COLS], U32, align_bytes=64)
        js = keep.tile([P, 16, 2, COLS], U8, align_bytes=64)
        o_sb = keep.tile([P, B, L, L], F32)

        make_identity(nc, ident[:])
        nc.sync.dma_start(out=x_sb[:], in_=seq_out.flatten_outer_dims())
        nc.gpsimd.memset(bias_rows[:], 0.0)
        nc.gpsimd.memset(xs[:].bitcast(I32), 0)
        nc.scalar.dma_start(out=bias_rows[0:8, :], in_=b_proj.rearrange("(r c) -> r c", c=P))
        nc.scalar.dma_start(out=bias_rows[8:9, :], in_=b_out.rearrange("(r c) -> r c", c=P))

        def load_piece(m, c, g):
            raw = wraw.tile([P, 4, 512], BF16, name="raw", tag="raw")
            rows = W_proj[H * m + 512 * g : H * m + 512 * g + 512, 512 * c : 512 * c + 512]
            nc.sync.dma_start(out=raw[:], in_=rows.rearrange("(t p) n -> p t n", p=P))
            return raw

        def pack_half(raw, grp, piece, half, on_vector):
            m, c, g = piece
            cols = slice(256 * half, 256 * half + 256)
            dst = grp[:, cols, :].rearrange("p (c i) t -> p c t i", i=4)
            src = raw[:, :, cols].rearrange("p t (c i) -> p c t i", i=4)
            if on_vector:
                nc.vector.tensor_copy(out=dst, in_=src)
            else:
                nc.scalar.copy(out=dst, in_=src)
            col0 = 512 * c + 256 * half
            nc.vector.quantize_mx(
                out=wc[m][:, g, col0 : col0 + 256].bitcast(FP8X4),
                scales=ws[m][:, g, col0 : col0 + 256],
                in_=grp[:, cols, :].rearrange("p n t -> p (n t)"),
            )

        def group_tile():
            grp = wgrp.tile([P, 512, 4], BF16, align_bytes=64, name="grp", tag="grp")
            return grp

        def pack_piece(raw, m, c, g, on_vector):
            grp = group_tile()
            for half in range(2):
                pack_half(raw, grp, (m, c, g), half, on_vector)

        first = [(0, 0, 0), (0, 0, 1), (1, 0, 0), (1, 0, 1), (2, 0, 0), (2, 0, 1)]
        second = [(0, 1, 0), (0, 1, 1), (1, 1, 0), (1, 1, 1), (2, 1, 0), (2, 1, 1)]
        raws = [load_piece(m, c, g) for (m, c, g) in first]

        for g in range(2):
            xt = psum.tile([P, 4, P], BF16, name="xt", tag="u")
            for t in range(4):
                k0 = 512 * g + P * t
                nc.tensor.transpose(xt[:, t, :], x_sb[:, k0 : k0 + P], ident[:])
            nc.scalar.copy(
                out=xg[:, g].rearrange("p l (b t) -> p l b t", b=B),
                in_=xt[:].rearrange("p t (b l) -> p l b t", b=B),
            )
        bt = psum.tile([P, P], BF16, name="bt", tag="u")
        nc.tensor.transpose(bt[:], bias_rows[:], ident[:])
        nc.vector.tensor_copy(out=bias[:], in_=bt[:, 0:16])

        def quantise_x():
            nc.vector.quantize_mx(
                out=xc[:].rearrange("p g r -> p (g r)").bitcast(FP8X4),
                scales=xs[:].rearrange("p g r -> p (g r)"),
                in_=xg[:].rearrange("p g l k -> p (g l k)"),
            )

        def expand_x(engine, i, k):
            for g in range(2):
                engine.tensor_copy(
                    out=xec[:, g, Q * i : Q * k].bitcast(I32),
                    in_=xc[:, g, Q * B * i : Q * B * k]
                    .bitcast(I32)
                    .rearrange("p (l b) -> p l b", b=B)
                    .unsqueeze(2)
                    .to_broadcast([P, Q * (k - i), Q, B]),
                )
                engine.tensor_copy(
                    out=xes[:, g, Q * i : Q * k].rearrange("p l m b -> p l (m b)").bitcast(I32),
                    in_=xs[:, g, Q * B * i : Q * B * k]
                    .bitcast(I32)
                    .unsqueeze(2)
                    .to_broadcast([P, Q * (k - i), Q]),
                )

        def product(blk):
            i, j = BLOCKS[blk]
            pr = prod.tile([P, 2, Q, Q, B * 4], BF16, align_bytes=64, name="pr", tag="pr")
            for g in range(2):
                nc.vector.tensor_tensor(
                    out=pr[:, g],
                    in0=xg[:, g, Q * i : Q * i + Q, :].unsqueeze(2).to_broadcast([P, Q, Q, B * 4]),
                    in1=xg[:, g, Q * j : Q * j + Q, :].unsqueeze(1).to_broadcast([P, Q, Q, B * 4]),
                    op=ALU.mult,
                )
            nc.vector.quantize_mx(
                out=pc[:, blk].rearrange("p g c -> p (g c)").bitcast(FP8X4),
                scales=ps[:, blk].rearrange("p g c -> p (g c)"),
                in_=pr[:].rearrange("p g a m k -> p (g a m k)"),
            )

        def tables(gh):
            for table, m in ((tab_c, 2), (tab_a, 1)):
                tp = psum_o.tile([P, 4, P], F32, name="tp", tag="o")
                for t in range(4):
                    h0 = 512 * gh + P * t
                    for g in range(2):
                        nc.tensor.matmul_mx(
                            out=tp[:, t, :],
                            lhsT=wc[m][:, g, h0 : h0 + P].bitcast(FP8X4),
                            lhsT_scale=ws[m][:, g, h0 : h0 + P],
                            rhs=xc[:, g, :].bitcast(FP8X4),
                            rhs_scale=xs[:, g, :],
                            start=(g == 0),
                            stop=(g == 1),
                        )
                for t in range(4):
                    plane = 4 * gh + t
                    nc.scalar.activation(
                        out=table[:, plane, :],
                        in_=tp[:, t, :],
                        func=ACTF.Identity,
                        bias=bias[:, plane : plane + 1],
                        scale=1.0,
                    )
            if any(gh == half for (blk, half) in DERIVED):
                nc.vector.tensor_tensor(
                    out=tab_e[:, gh],
                    in0=tab_c[:, 4 * gh : 4 * gh + 4, :].rearrange("p (q u) k -> p q k u", u=2),
                    in1=tab_a[:, 4 * gh : 4 * gh + 4, :].rearrange("p (q u) k -> p q k u", u=2),
                    op=ALU.subtract,
                )

        def pack_w_out():
            nc.scalar.copy(out=grp_o[:], in_=raw_o[:].rearrange("p (g t) n -> p g n t", t=4))
            nc.vector.quantize_mx(
                out=oc[:].rearrange("p g n -> p (g n)").bitcast(FP8X4),
                scales=os_[:].rearrange("p g n -> p (g n)"),
                in_=grp_o[:].rearrange("p g n t -> p (g n t)"),
            )

        def of_minor(table, plane, j, majors=Q):
            view = table[:, plane : plane + 2, Q * B * j : Q * B * (j + 1)].rearrange("p u k -> p k u")
            return view.unsqueeze(1).to_broadcast([P, majors, Q * B, 2])

        def pair_sums(blk, gh, m_in):
            i = BLOCKS[blk][0]
            banks = []
            for q in range(2):
                bank = psum.tile([P, 2, COLS], F32, name="bank", tag="u")
                for u in range(2):
                    h0 = 512 * gh + P * (2 * q + u)
                    for g in range(2):
                        nc.tensor.matmul_mx(
                            out=bank[:, u, :],
                            lhsT=wc[0][:, g, h0 : h0 + P].bitcast(FP8X4),
                            lhsT_scale=ws[0][:, g, h0 : h0 + P],
                            rhs=pc[:, blk, g, :].bitcast(FP8X4),
                            rhs_scale=ps[:, blk, g, :],
                            start=(g == 0),
                            stop=False,
                        )
                    for g in range(2):
                        nc.tensor.matmul_mx(
                            out=bank[:, u, :],
                            lhsT=wc[m_in][:, g, h0 : h0 + P].bitcast(FP8X4),
                            lhsT_scale=ws[m_in][:, g, h0 : h0 + P],
                            rhs=xec[:, g, Q * i : Q * i + Q].rearrange("p a m b -> p (a m b)").bitcast(FP8X4),
                            rhs_scale=xes[:, g, Q * i : Q * i + Q].rearrange("p a m b -> p (a m b)"),
                            start=False,
                            stop=(g == 1),
                        )
                banks.append(bank)
            return banks

        def squash(banks, addend, tau, gh, splits):
            majors = Q // splits
            groups = [slice(COLS // splits * s, COLS // splits * (s + 1)) for s in range(splits)]
            z = zpool.tile([P, 2, COLS, 2], F32, name="z", tag="z")
            pj = jpool.tile([P, COLS, 4], BF16, align_bytes=64, name="pj", tag="pj")
            for q in range(2):
                for cols in groups:
                    nc.vector.tensor_tensor(
                        out=z[:, q, cols, :].rearrange("p (a k) u -> p a k u", a=majors),
                        in0=banks[q][:, :, cols].rearrange("p u (a k) -> p a k u", a=majors),
                        in1=addend(q, majors, cols),
                        op=ALU.add,
                    )
                    if q == 1:
                        nc.scalar.activation(
                            out=pj[:, cols, :].rearrange("p c (q u) -> p c q u", u=2),
                            in_=z[:, :, cols, :].rearrange("p q c u -> p c q u"),
                            func=ACTF.Tanh,
                        )
            for cols in groups:
                nc.vector.quantize_mx(
                    out=jc[:, tau, gh, cols].bitcast(FP8X4),
                    scales=js[:, tau, gh, cols],
                    in_=pj[:, cols, :].rearrange("p c t -> p (c t)"),
                )

        def sums(blk, mirrored, gh):
            if not mirrored:
                return pair_sums(blk, gh, 1)
            if (blk, gh) not in DERIVED:
                return pair_sums(blk, gh, 2)
            return None

        def unit(tau, blk, mirrored, gh, banks, splits):
            i, j = BLOCKS[blk]
            if mirrored and (blk, gh) in DERIVED:
                s2 = spool.tile([P, 2, COLS, 2], F32, name="s2", tag="s2")
                for q in range(2):
                    nc.vector.tensor_tensor(
                        out=s2[:, q].rearrange("p (a m b) u -> p a m b u", a=Q, m=Q),
                        in0=tab_e[:, gh, q, Q * B * i : Q * B * (i + 1), :]
                        .rearrange("p (a b) u -> p a b u", b=B)
                        .unsqueeze(2)
                        .to_broadcast([P, Q, Q, B, 2]),
                        in1=of_minor(tab_a, 4 * gh + 2 * q, j)
                        .rearrange("p a (m b) u -> p a m b u", b=B),
                        op=ALU.add,
                    )

                def addend(q, majors, cols):
                    return s2[:, q, cols, :].rearrange("p (a k) u -> p a k u", a=majors)

            else:
                table = tab_a if mirrored else tab_c

                def addend(q, majors, cols):
                    return of_minor(table, 4 * gh + 2 * q, j, majors)

            squash(banks, addend, tau, gh, splits)

        def labels(tau, blk, mirrored, splits):
            i, j = BLOCKS[blk]
            width = COLS // splits
            for s in range(splits):
                ob = psum_o.tile([P, COLS], F32, name="ob", tag="o")
                cols = slice(width * s, width * (s + 1))
                for gh in range(2):
                    nc.tensor.matmul_mx(
                        out=ob[:, 0:width],
                        lhsT=oc[:, gh, :].bitcast(FP8X4),
                        lhsT_scale=os_[:, gh, :],
                        rhs=jc[:, tau, gh, cols].bitcast(FP8X4),
                        rhs_scale=js[:, tau, gh, cols],
                        start=(gh == 0),
                        stop=(gh == 1),
                    )
                rows = Q // splits
                if mirrored:
                    src = ob[:].rearrange("p (a m b) -> p b m a", a=Q, m=Q)
                    dst = o_sb[:, :, Q * j : Q * j + Q, Q * i : Q * i + Q]
                else:
                    src = ob[:, 0:width].rearrange("p (a m b) -> p b a m", a=rows, m=Q)
                    dst = o_sb[:, :, Q * i + rows * s : Q * i + rows * (s + 1), Q * j : Q * j + Q]
                nc.scalar.activation(
                    out=dst,
                    in_=src,
                    func=ACTF.Identity,
                    bias=bias[:, 8:9],
                    scale=1.0,
                )
                if j == 3 and not mirrored:
                    row0 = Q * i + rows * s
                    nc.sync.dma_start(
                        out=out[:, :, row0 : row0 + rows, :].rearrange("b k i j -> k b (i j)"),
                        in_=o_sb[:, :, row0 : row0 + rows, :].rearrange("p b i j -> p b (i j)"),
                    )

        taus = {}
        for blk, (i, j) in enumerate(BLOCKS):
            taus[(blk, False)] = len(taus)
            if i != j:
                taus[(blk, True)] = len(taus)

        def tiles(blks, gh):
            return [(blk, mir, gh) for blk in blks for mir in (False, True) if (blk, mir) in taus]

        early = range(6)
        order = tiles(early, 0) + tiles(early, 1)
        for blk in range(6, 10):
            order += tiles([blk], 0) + tiles([blk], 1)

        pack_piece(raws[0], *first[0], on_vector=True)
        quantise_x()
        pack_piece(raws[1], *first[1], on_vector=False)
        product(0)
        expand_x(nc.vector, 0, 1)
        expand_x(nc.gpsimd, 1, 4)
        pack_piece(raws[2], *first[2], on_vector=False)
        pack_piece(raws[3], *first[3], on_vector=False)
        product(1)
        banks_of = {}
        for n in range(2):
            banks_of[n] = sums(*order[n])
        pack_piece(raws[4], *first[4], on_vector=False)
        pack_piece(raws[5], *first[5], on_vector=False)
        raws2 = [load_piece(m, c, g) for (m, c, g) in second]
        nc.sync.dma_start(out=raw_o[:], in_=W_out.rearrange("(a p) n -> p a n", p=P))
        tables(0)

        made = set([0, 1])
        grps = {}
        halves_done = 0
        for n, (blk, mir, gh) in enumerate(order):
            for blk2, mir2, gh2 in order[n : n + 3]:
                if blk2 not in made:
                    product(blk2)
                    made.add(blk2)
            if n not in banks_of:
                banks_of[n] = sums(blk, mir, gh) or banks_of[n - 1]
            splits = 2 if n == len(order) - 1 else 1
            unit(taus[(blk, mir)], blk, mir, gh, banks_of[n], splits)
            while halves_done < min(12, 4 * (n + 1) // 3):
                k, half = divmod(halves_done, 2)
                if half == 0:
                    grps[k] = group_tile()
                pack_half(raws2[k], grps[k], second[k], half, on_vector=False)
                halves_done += 1
            if n == 8:
                tables(1)
                pack_w_out()
            if gh == 1:
                labels(taus[(blk, mir)], blk, mir, splits)
